import numpy as np
import ml_dtypes


def mxq(x, axis, fmt="e4m3"):
    dtype, down = {"e4m3": (ml_dtypes.float8_e4m3fn, 7), "e5m2": (ml_dtypes.float8_e5m2, 14)}[fmt]
    v = np.moveaxis(np.asarray(x, np.float32).astype(ml_dtypes.bfloat16).astype(np.float64), axis, -1)
    blocks = v.reshape(v.shape[:-1] + (-1, 32))
    amax = np.abs(blocks).max(-1, keepdims=True)
    byte = np.maximum(np.where(amax > 0, np.frexp(amax)[1] - 1 + 127, 0) - down, 1)
    scale = np.exp2(byte - 127.0)
    codes = (blocks / scale).astype(np.float32).astype(dtype).astype(np.float64)
    return np.moveaxis((codes * scale).reshape(v.shape), -1, axis)


WIDE = False


def mx_kscale(k):
    if not WIDE:
        return np.ones(k)
    levels = np.array([10, -10, 5, -5, 0])
    a = np.random.permutation(np.resize(levels, k // 512 * 4)).reshape(k // 512, 4)
    idx = np.arange(k)
    return np.exp2(a[idx // 512, idx % 128 // 32])


BF16 = ml_dtypes.bfloat16


def bf(x):
    return np.asarray(x, np.float32).astype(BF16)


def f64(x):
    return np.asarray(x).astype(np.float64)


B, S, E, H, DH, F = 4, 128, 1024, 8, 128, 4096
HD = H * DH
EPS = 1e-6
ERF_CLIP = 6.0
ERF_TERMS = 100


def layer_norm(x, g, b):
    m = x.mean(-1, keepdims=True)
    v = np.square(x - m).mean(-1, keepdims=True)
    return (x - m) * (1.0 / np.sqrt(v + EPS)) * g + b


def erf(v):
    a = np.clip(v, -ERF_CLIP, ERF_CLIP)
    a2 = 2.0 * a * a
    term = a.copy()
    tot = a.copy()
    for n in range(1, ERF_TERMS):
        term = term * a2 / (2.0 * n + 1.0)
        tot = tot + term
    return 2.0 / np.sqrt(np.pi) * np.exp(-a * a) * tot


def gelu(v):
    return 0.5 * v * (1.0 + erf(v / np.sqrt(2.0)))


def setup_inputs():
    s = mx_kscale(HD).reshape(H, DH)
    t = mx_kscale(E)
    return {"h_attn": bf(0.35 * np.random.standard_normal((B, S, H, DH)) * s),
            "Wo": bf((np.random.standard_normal((H, DH, E)) + 0.5 * np.random.standard_normal((H, DH, 1))) / np.sqrt(HD) / s[:, :, None]),
            "gamma2": bf((1.0 + 0.1 * np.random.standard_normal(E)) * t),
            "beta2": bf(0.1 * np.random.standard_normal(E) * t),
            "Wg": bf(np.random.standard_normal((E, F)) / np.sqrt(E) / t[:, None]),
            "Wu": bf(np.random.standard_normal((E, F)) / np.sqrt(E) / t[:, None])}


def reference(h_attn, Wo, gamma2, beta2, Wg, Wu):
    attn_out = mxq(f64(h_attn).reshape(B, S, HD), 2, "e4m3") @ mxq(f64(Wo).reshape(HD, E), 0, "e4m3")
    z = layer_norm(attn_out, f64(gamma2), f64(beta2))
    zq = mxq(z, 2, "e4m3")
    gate = gelu(zq @ mxq(f64(Wg), 0, "e4m3"))
    return gate * (zq @ mxq(f64(Wu), 0, "e4m3"))

@@ -1,0 +1,249 @@
+from contextlib import ExitStack
+
+import concourse.mybir as mybir
+from concourse.masks import make_identity
+
+F32 = mybir.dt.float32
+BF16 = mybir.dt.bfloat16
+U32 = mybir.dt.uint32
+U8 = mybir.dt.uint8
+FP8X4 = mybir.dt.float8_e4m3fn_x4
+ACT = mybir.ActivationFunctionType
+ALU = mybir.AluOpType
+
+P = 128
+PACK = 4
+K_PASS = P * PACK
+TOKENS = 512
+TOK_TILES = TOKENS // P
+E = 1024
+F = 4096
+PASSES = E // K_PASS
+N_TILE = 512
+CHUNK = 1024
+TILES_PER_CHUNK = CHUNK // N_TILE
+CHUNKS = F // CHUNK
+E_BLOCKS = E // P
+RUN = 4
+EPS = 1e-6
+RAW_BUFS = 5
+
+FLOPS = 2 * TOKENS * E * (E + 2 * F)
+
+
+def regroup(copy, grouped, rows):
+    copy(
+        out=grouped.rearrange("p (c i t) -> p c t i", i=RUN, t=PACK),
+        in_=rows.rearrange("p t (c i) -> p c t i", i=RUN),
+    )
+
+
+def tile_selfdecoderblock_pb_kernel(tc, h_attn, Wo, gamma2, beta2, Wg, Wu, out):
+    nc = tc.nc
+    h_rows_dram = h_attn.rearrange("b s h d -> b s (h d)")
+    wo_dram = Wo.rearrange("h d e -> (h d) e")
+    out_dram = out.rearrange("b s f -> s b f")
+
+    with ExitStack() as ctx:
+        keep = ctx.enter_context(tc.tile_pool(name="keep", bufs=1))
+        raw_pool = ctx.enter_context(tc.tile_pool(name="raw", bufs=RAW_BUFS))
+        stage = ctx.enter_context(tc.tile_pool(name="stage", bufs=6))
+        weights = ctx.enter_context(tc.tile_pool(name="weights", bufs=5))
+        psum = ctx.enter_context(tc.psum_pool(name="psum", bufs=8))
+
+        def bank(shape, dtype):
+            return psum.tile(shape, dtype, name="bank")
+
+        def load_wo():
+            raw = raw_pool.tile([P, PASSES, PACK, CHUNK], BF16, name="raw")
+            for g in range(PASSES):
+                for u in range(2):
+                    first = g * K_PASS + u * 2 * P
+                    nc.sync.dma_start(
+                        out=raw[:, g, 2 * u : 2 * u + 2, :],
+                        in_=wo_dram[first : first + 2 * P, :].rearrange("(p e) n -> p e n", e=2),
+                    )
+            return raw
+
+        def load_gate_or_up(index):
+            w, c = chunk_order[index]
+            raw = raw_pool.tile([P, PASSES, PACK, CHUNK], BF16, name="raw")
+            for g in range(PASSES):
+                nc.sync.dma_start(
+                    out=raw[:, g],
+                    in_=w[g * K_PASS : (g + 1) * K_PASS, c * CHUNK : (c + 1) * CHUNK].rearrange("(t p) n -> p t n", p=P),
+                )
+            return raw
+
+        def quantise_weight_chunk(raw):
+            codes = weights.tile([P, PASSES, CHUNK], U32, name="codes", align_bytes=64)
+            scales = weights.tile([P, PASSES, CHUNK], U8, name="scales", align_bytes=64)
+            for i in range(TILES_PER_CHUNK):
+                cols = slice(i * N_TILE, (i + 1) * N_TILE)
+                for g in range(PASSES):
+                    grouped = stage.tile([P, N_TILE * PACK], BF16, name="grouped", align_bytes=64)
+                    copy = nc.vector.tensor_copy if g == 0 else nc.scalar.copy
+                    regroup(copy, grouped[:], raw[:, g, :, cols])
+                    nc.vector.quantize_mx(
+                        out=codes[:, g, cols].bitcast(FP8X4), scales=scales[:, g, cols], in_=grouped[:]
+                    )
+            return codes, scales
+
+        def product(acc, left, left_cols, right, right_cols, g):
+            nc.tensor.matmul_mx(
+                out=acc,
+                lhsT=left[0][:, g, left_cols].bitcast(FP8X4),
+                lhsT_scale=left[1][:, g, left_cols],
+                rhs=right[0][:, g, right_cols].bitcast(FP8X4),
+                rhs_scale=right[1][:, g, right_cols],
+                start=(g == 0),
+                stop=(g == PASSES - 1),
+            )
+
+        chunk_order = [(w, c) for c in range(CHUNKS) for w in (Wg, Wu)]
+
+        ident_f32 = keep.tile([P, P], F32, name="ident_f32")
+        make_identity(nc, ident_f32[:])
+        ident_bf16 = keep.tile([P, P], BF16, name="ident_bf16")
+        make_identity(nc, ident_bf16[:])
+        eps = keep.tile([P, 1], F32, name="eps")
+        nc.vector.memset(eps[:], EPS)
+        warm = keep.tile([P, 2], F32, name="warm")
+        nc.scalar.activation(out=warm[:, 0:1], in_=eps[:], func=ACT.Sqrt)
+
+        z_codes = keep.tile([P, PASSES, TOKENS], U32, name="z_codes", align_bytes=64)
+        z_scales = keep.tile([P, PASSES, TOKENS], U8, name="z_scales", align_bytes=64)
+
+        with tc.tile_pool(name="early", bufs=1) as early:
+            h_rows = []
+            for m in range(TOK_TILES):
+                rows = early.tile([P, E], BF16, name="h_rows%d" % m)
+                nc.sync.dma_start(out=rows[:], in_=h_rows_dram[m])
+                h_rows.append(rows)
+            wo_raw = load_wo()
+            gb_rows = early.tile([P, P], BF16, name="gb_rows")
+            nc.vector.memset(gb_rows[:], 0.0)
+            nc.scalar.dma_start(out=gb_rows[0:E_BLOCKS, :], in_=gamma2.rearrange("(r c) -> r c", c=P))
+            nc.scalar.dma_start(out=gb_rows[E_BLOCKS : 2 * E_BLOCKS, :], in_=beta2.rearrange("(r c) -> r c", c=P))
+            raws = [load_gate_or_up(index) for index in range(RAW_BUFS - 1)]
+
+            h_codes = early.tile([P, PASSES, TOKENS], U32, name="h_codes", align_bytes=64)
+            h_scales = early.tile([P, PASSES, TOKENS], U8, name="h_scales", align_bytes=64)
+            for m in range(TOK_TILES):
+                toks = slice(m * P, (m + 1) * P)
+                words = bank([P, PASSES * 2, P], F32)
+                for q in range(PASSES * 2):
+                    nc.tensor.transpose(
+                        words[:, q, :], h_rows[m][:].bitcast(F32)[:, q * P : (q + 1) * P], ident_f32[:]
+                    )
+                h_grouped = early.tile([P, PASSES, P * PACK], BF16, name="h_grouped%d" % m, align_bytes=64)
+                copy = nc.vector.tensor_copy if m % 2 == 0 else nc.scalar.copy
+                copy(
+                    out=h_grouped[:].bitcast(F32).rearrange("p g (r u) -> p g r u", u=2),
+                    in_=words[:].rearrange("p (g u) r -> p g r u", u=2),
+                )
+                for g in range(PASSES):
+                    nc.vector.quantize_mx(
+                        out=h_codes[:, g, toks].bitcast(FP8X4), scales=h_scales[:, g, toks], in_=h_grouped[:, g, :]
+                    )
+
+            gb_bank = bank([P, P], BF16)
+            nc.tensor.transpose(gb_bank[:], gb_rows[:], ident_bf16[:])
+            gain_bias = early.tile([P, 2 * E_BLOCKS], F32, name="gain_bias")
+            nc.vector.tensor_copy(out=gain_bias[:], in_=gb_bank[:, 0 : 2 * E_BLOCKS])
+
+            wo = quantise_weight_chunk(wo_raw)
+            raws.append(load_gate_or_up(RAW_BUFS - 1))
+            a = {}
+            for g in range(PASSES):
+                for m in range(TOK_TILES):
+                    for n in range(TILES_PER_CHUNK):
+                        if g == 0:
+                            a[m, n] = bank([P, N_TILE], F32)
+                        product(
+                            a[m, n][:],
+                            (h_codes, h_scales),
+                            slice(m * P, (m + 1) * P),
+                            wo,
+                            slice(n * N_TILE, (n + 1) * N_TILE),
+                            g,
+                        )
+
+            stats = early.tile([P, TOK_TILES, TILES_PER_CHUNK, 6], F32, name="stats")
+            mean_var = early.tile([P, TOK_TILES, 2], F32, name="mean_var")
+            std = early.tile([P, TOK_TILES], F32, name="std")
+            rstd = early.tile([P, TOK_TILES], F32, name="rstd")
+            shift = early.tile([P, TOK_TILES], F32, name="shift")
+            normed = []
+            for m in range(TOK_TILES):
+                one = slice(m, m + 1)
+                for n in range(TILES_PER_CHUNK):
+                    nc.vector.bn_stats(out=stats[:, m, n, :], in_=a[m, n][:])
+                nc.vector.bn_aggr(out=mean_var[:, m, :], in_=stats[:, m].rearrange("p n s -> p (n s)"))
+                nc.scalar.activation(out=std[:, one], in_=mean_var[:, m, 1:2], func=ACT.Sqrt, bias=eps[:], scale=1.0)
+                nc.vector.reciprocal(out=rstd[:, one], in_=std[:, one])
+                nc.vector.scalar_tensor_tensor(
+                    out=shift[:, one], in0=mean_var[:, m, 0:1], scalar=-1.0, in1=rstd[:, one], op0=ALU.mult, op1=ALU.mult
+                )
+                x = early.tile([P, E], F32, name="normed%d" % m)
+                for n in range(TILES_PER_CHUNK):
+                    nc.scalar.activation(
+                        out=x[:, n * N_TILE : (n + 1) * N_TILE],
+                        in_=a[m, n][:],
+                        func=ACT.Identity,
+                        scale=rstd[:, one],
+                        bias=shift[:, one],
+                    )
+                normed.append(x)
+
+            z_planes = early.tile([P, E_BLOCKS, TOKENS], BF16, name="z_planes")
+            for r in range(E_BLOCKS):
+                flipped = bank([P, TOKENS], F32)
+                for m in range(TOK_TILES):
+                    nc.tensor.transpose(
+                        flipped[:, m * P : (m + 1) * P], normed[m][:, r * P : (r + 1) * P], ident_f32[:]
+                    )
+                gain = gain_bias[:, r : r + 1]
+                bias = gain_bias[:, E_BLOCKS + r : E_BLOCKS + r + 1]
+                if r % 2 == 0:
+                    nc.scalar.activation(out=z_planes[:, r, :], in_=flipped[:], func=ACT.Identity, scale=gain, bias=bias)
+                else:
+                    nc.vector.tensor_scalar(
+                        out=z_planes[:, r, :], in0=flipped[:], scalar1=gain, scalar2=bias, op0=ALU.mult, op1=ALU.add
+                    )
+            nc.scalar.activation(out=warm[:, 1:2], in_=z_planes[:, E_BLOCKS - 2, 0:1], func=ACT.Gelu)
+            for g in range(PASSES):
+                z_grouped = early.tile([P, TOKENS * PACK], BF16, name="z_grouped%d" % g, align_bytes=64)
+                regroup(nc.vector.tensor_copy, z_grouped[:], z_planes[:, g * PACK : (g + 1) * PACK, :])
+                nc.vector.quantize_mx(out=z_codes[:, g, :].bitcast(FP8X4), scales=z_scales[:, g, :], in_=z_grouped[:])
+
+        z = (z_codes, z_scales)
+        late = ctx.enter_context(tc.tile_pool(name="late", bufs=1, reuse_waits="tile"))
+        for c in range(CHUNKS):
+            quantised = []
+            for index in (2 * c, 2 * c + 1):
+                quantised.append(quantise_weight_chunk(raws[index]))
+                if index + RAW_BUFS < len(chunk_order):
+                    raws.append(load_gate_or_up(index + RAW_BUFS))
+            wg, wu = quantised
+            gates = {}
+            for i in range(TILES_PER_CHUNK):
+                cols = slice(i * N_TILE, (i + 1) * N_TILE)
+                for m in range(TOK_TILES):
+                    acc = bank([P, N_TILE], F32)
+                    for g in range(PASSES):
+                        product(acc[:], z, slice(m * P, (m + 1) * P), wg, cols, g)
+                    gates[i, m] = late.tile([P, N_TILE], F32, name="gate", bufs=10)
+                    nc.scalar.activation(out=gates[i, m][:], in_=acc[:], func=ACT.Gelu)
+            for i in range(TILES_PER_CHUNK):
+                cols = slice(i * N_TILE, (i + 1) * N_TILE)
+                out_cols = slice(c * CHUNK + i * N_TILE, c * CHUNK + (i + 1) * N_TILE)
+                for pair in range(TOK_TILES // 2):
+                    result = late.tile([P, 2, N_TILE], F32, name="result", bufs=4)
+                    for half in range(2):
+                        m = 2 * pair + half
+                        acc = bank([P, N_TILE], F32)
+                        for g in range(PASSES):
+                            product(acc[:], z, slice(m * P, (m + 1) * P), wu, cols, g)
+                        nc.vector.tensor_tensor(out=result[:, half, :], in0=gates[i, m][:], in1=acc[:], op=ALU.mult)
+                    nc.sync.dma_start(out=out_dram[:, 2 * pair : 2 * pair + 2, out_cols], in_=result[:])

@@ -22,11 +22,13 @@ PASSES = E // K_PASS
 N_TILE = 512
 CHUNK = 1024
 TILES_PER_CHUNK = CHUNK // N_TILE
-CHUNKS = F // CHUNK
+F_TILES = F // N_TILE
 E_BLOCKS = E // P
 RUN = 4
 EPS = 1e-6
 RAW_BUFS = 5
+GATE = 0
+UP = 1
 
 FLOPS = 2 * TOKENS * E * (E + 2 * F)
 
@@ -43,12 +45,14 @@ def tile_selfdecoderblock_pb_kernel(tc, h_attn, Wo, gamma2, beta2, Wg, Wu, out):
     h_rows_dram = h_attn.rearrange("b s h d -> b s (h d)")
     wo_dram = Wo.rearrange("h d e -> (h d) e")
     out_dram = out.rearrange("b s f -> s b f")
+    chunk_order = [(w, c) for c in range(F // CHUNK) for w in (Wg, Wu)]
 
     with ExitStack() as ctx:
+        ctx.enter_context(tc.manual_schedule())
         keep = ctx.enter_context(tc.tile_pool(name="keep", bufs=1))
         raw_pool = ctx.enter_context(tc.tile_pool(name="raw", bufs=RAW_BUFS))
-        stage = ctx.enter_context(tc.tile_pool(name="stage", bufs=6))
-        weights = ctx.enter_context(tc.tile_pool(name="weights", bufs=5))
+        stage = ctx.enter_context(tc.tile_pool(name="stage", bufs=10))
+        weights = ctx.enter_context(tc.tile_pool(name="weights", bufs=6))
         psum = ctx.enter_context(tc.psum_pool(name="psum", bufs=8))
 
         def bank(shape, dtype):
@@ -65,29 +69,28 @@ def tile_selfdecoderblock_pb_kernel(tc, h_attn, Wo, gamma2, beta2, Wg, Wu, out):
                     )
             return raw
 
-        def load_gate_or_up(index):
-            w, c = chunk_order[index]
-            raw = raw_pool.tile([P, PASSES, PACK, CHUNK], BF16, name="raw")
-            for g in range(PASSES):
-                nc.sync.dma_start(
-                    out=raw[:, g],
-                    in_=w[g * K_PASS : (g + 1) * K_PASS, c * CHUNK : (c + 1) * CHUNK].rearrange("(t p) n -> p t n", p=P),
-                )
-            return raw
+        raws = []
 
-        def quantise_weight_chunk(raw):
-            codes = weights.tile([P, PASSES, CHUNK], U32, name="codes", align_bytes=64)
-            scales = weights.tile([P, PASSES, CHUNK], U8, name="scales", align_bytes=64)
-            for i in range(TILES_PER_CHUNK):
-                cols = slice(i * N_TILE, (i + 1) * N_TILE)
+        def load_chunks(count):
+            for w, c in chunk_order[len(raws) : count]:
+                raw = raw_pool.tile([P, PASSES, PACK, CHUNK], BF16, name="raw")
                 for g in range(PASSES):
-                    grouped = stage.tile([P, N_TILE * PACK], BF16, name="grouped", align_bytes=64)
-                    copy = nc.vector.tensor_copy if g == 0 else nc.scalar.copy
-                    regroup(copy, grouped[:], raw[:, g, :, cols])
-                    nc.vector.quantize_mx(
-                        out=codes[:, g, cols].bitcast(FP8X4), scales=scales[:, g, cols], in_=grouped[:]
+                    nc.sync.dma_start(
+                        out=raw[:, g],
+                        in_=w[g * K_PASS : (g + 1) * K_PASS, c * CHUNK : (c + 1) * CHUNK].rearrange(
+                            "(t p) n -> p t n", p=P
+                        ),
                     )
-            return codes, scales
+                raws.append(raw)
+
+        def copy_unit(copy, raw, g, tile_in_chunk):
+            grouped = stage.tile([P, N_TILE * PACK], BF16, name="grouped", align_bytes=64)
+            regroup(copy, grouped[:], raw[:, g, :, tile_in_chunk * N_TILE : (tile_in_chunk + 1) * N_TILE])
+            return grouped
+
+        def quantise_unit(grouped, operand, g, cols):
+            codes, scales = operand
+            nc.vector.quantize_mx(out=codes[:, g, cols].bitcast(FP8X4), scales=scales[:, g, cols], in_=grouped[:])
 
         def product(acc, left, left_cols, right, right_cols, g):
             nc.tensor.matmul_mx(
@@ -100,7 +103,24 @@ def tile_selfdecoderblock_pb_kernel(tc, h_attn, Wo, gamma2, beta2, Wg, Wu, out):
                 stop=(g == PASSES - 1),
             )
 
-        chunk_order = [(w, c) for c in range(CHUNKS) for w in (Wg, Wu)]
+        def tokens(m):
+            return slice(m * P, (m + 1) * P)
+
+        grouped_units = {}
+        moving = {}
+
+        def copy_weight_unit(b, j, g):
+            copy = nc.scalar.copy if g == 0 else nc.vector.tensor_copy
+            raw = raws[2 * (j // TILES_PER_CHUNK) + b]
+            grouped_units[b, j, g] = copy_unit(copy, raw, g, j % TILES_PER_CHUNK)
+
+        def quantise_weight_tile(b, j):
+            moving[b, j] = (
+                weights.tile([P, PASSES, N_TILE], U32, name="codes", align_bytes=64),
+                weights.tile([P, PASSES, N_TILE], U8, name="scales", align_bytes=64),
+            )
+            for g in range(PASSES):
+                quantise_unit(grouped_units[b, j, g], moving[b, j], g, slice(0, N_TILE))
 
         ident_f32 = keep.tile([P, P], F32, name="ident_f32")
         make_identity(nc, ident_f32[:])
@@ -109,10 +129,10 @@ def tile_selfdecoderblock_pb_kernel(tc, h_attn, Wo, gamma2, beta2, Wg, Wu, out):
         eps = keep.tile([P, 1], F32, name="eps")
         nc.vector.memset(eps[:], EPS)
         warm = keep.tile([P, 2], F32, name="warm")
-        nc.scalar.activation(out=warm[:, 0:1], in_=eps[:], func=ACT.Sqrt)
-
-        z_codes = keep.tile([P, PASSES, TOKENS], U32, name="z_codes", align_bytes=64)
-        z_scales = keep.tile([P, PASSES, TOKENS], U8, name="z_scales", align_bytes=64)
+        z = (
+            keep.tile([P, PASSES, TOKENS], U32, name="z_codes", align_bytes=64),
+            keep.tile([P, PASSES, TOKENS], U8, name="z_scales", align_bytes=64),
+        )
 
         with tc.tile_pool(name="early", bufs=1) as early:
             h_rows = []
@@ -121,30 +141,34 @@ def tile_selfdecoderblock_pb_kernel(tc, h_attn, Wo, gamma2, beta2, Wg, Wu, out):
                 nc.sync.dma_start(out=rows[:], in_=h_rows_dram[m])
                 h_rows.append(rows)
             wo_raw = load_wo()
+            load_chunks(RAW_BUFS - 1)
             gb_rows = early.tile([P, P], BF16, name="gb_rows")
             nc.vector.memset(gb_rows[:], 0.0)
             nc.scalar.dma_start(out=gb_rows[0:E_BLOCKS, :], in_=gamma2.rearrange("(r c) -> r c", c=P))
             nc.scalar.dma_start(out=gb_rows[E_BLOCKS : 2 * E_BLOCKS, :], in_=beta2.rearrange("(r c) -> r c", c=P))
-            raws = [load_gate_or_up(index) for index in range(RAW_BUFS - 1)]
+            nc.scalar.activation(out=warm[:, 0:1], in_=eps[:], func=ACT.Sqrt)
 
-            h_codes = early.tile([P, PASSES, TOKENS], U32, name="h_codes", align_bytes=64)
-            h_scales = early.tile([P, PASSES, TOKENS], U8, name="h_scales", align_bytes=64)
+            h = (
+                early.tile([P, PASSES, TOKENS], U32, name="h_codes", align_bytes=64),
+                early.tile([P, PASSES, TOKENS], U8, name="h_scales", align_bytes=64),
+            )
+            h_grouped = []
             for m in range(TOK_TILES):
-                toks = slice(m * P, (m + 1) * P)
                 words = bank([P, PASSES * 2, P], F32)
                 for q in range(PASSES * 2):
                     nc.tensor.transpose(
                         words[:, q, :], h_rows[m][:].bitcast(F32)[:, q * P : (q + 1) * P], ident_f32[:]
                     )
-                h_grouped = early.tile([P, PASSES, P * PACK], BF16, name="h_grouped%d" % m, align_bytes=64)
-                copy = nc.vector.tensor_copy if m % 2 == 0 else nc.scalar.copy
-                copy(
-                    out=h_grouped[:].bitcast(F32).rearrange("p g (r u) -> p g r u", u=2),
+                grouped = early.tile([P, PASSES, P * PACK], BF16, name="h_grouped%d" % m, align_bytes=64)
+                nc.scalar.copy(
+                    out=grouped[:].bitcast(F32).rearrange("p g (r u) -> p g r u", u=2),
                     in_=words[:].rearrange("p (g u) r -> p g r u", u=2),
                 )
+                h_grouped.append(grouped)
+            for m in range(TOK_TILES):
                 for g in range(PASSES):
                     nc.vector.quantize_mx(
-                        out=h_codes[:, g, toks].bitcast(FP8X4), scales=h_scales[:, g, toks], in_=h_grouped[:, g, :]
+                        out=h[0][:, g, tokens(m)].bitcast(FP8X4), scales=h[1][:, g, tokens(m)], in_=h_grouped[m][:, g, :]
                     )
 
             gb_bank = bank([P, P], BF16)
@@ -152,57 +176,76 @@ def tile_selfdecoderblock_pb_kernel(tc, h_attn, Wo, gamma2, beta2, Wg, Wu, out):
             gain_bias = early.tile([P, 2 * E_BLOCKS], F32, name="gain_bias")
             nc.vector.tensor_copy(out=gain_bias[:], in_=gb_bank[:, 0 : 2 * E_BLOCKS])
 
-            wo = quantise_weight_chunk(wo_raw)
-            raws.append(load_gate_or_up(RAW_BUFS - 1))
+            wo = (
+                early.tile([P, PASSES, E], U32, name="wo_codes", align_bytes=64),
+                early.tile([P, PASSES, E], U8, name="wo_scales", align_bytes=64),
+            )
+            wo_grouped = {}
+            for g in range(PASSES):
+                wo_grouped[g, 0] = copy_unit(nc.vector.tensor_copy, wo_raw, g, 0)
+                wo_grouped[g, 1] = copy_unit(nc.scalar.copy, wo_raw, g, 1)
+                if g > 0:
+                    quantise_unit(wo_grouped[g - 1, 1], wo, g - 1, slice(N_TILE, 2 * N_TILE))
+                quantise_unit(wo_grouped[g, 0], wo, g, slice(0, N_TILE))
+            quantise_unit(wo_grouped[PASSES - 1, 1], wo, PASSES - 1, slice(N_TILE, 2 * N_TILE))
+            load_chunks(RAW_BUFS)
             a = {}
             for g in range(PASSES):
-                for m in range(TOK_TILES):
-                    for n in range(TILES_PER_CHUNK):
+                for n in range(TILES_PER_CHUNK):
+                    for m in range(TOK_TILES):
                         if g == 0:
                             a[m, n] = bank([P, N_TILE], F32)
-                        product(
-                            a[m, n][:],
-                            (h_codes, h_scales),
-                            slice(m * P, (m + 1) * P),
-                            wo,
-                            slice(n * N_TILE, (n + 1) * N_TILE),
-                            g,
-                        )
+                        product(a[m, n][:], h, tokens(m), wo, slice(n * N_TILE, (n + 1) * N_TILE), g)
+
+            copy_weight_unit(GATE, 0, 0)
 
             stats = early.tile([P, TOK_TILES, TILES_PER_CHUNK, 6], F32, name="stats")
             mean_var = early.tile([P, TOK_TILES, 2], F32, name="mean_var")
             std = early.tile([P, TOK_TILES], F32, name="std")
             rstd = early.tile([P, TOK_TILES], F32, name="rstd")
             shift = early.tile([P, TOK_TILES], F32, name="shift")
-            normed = []
-            for m in range(TOK_TILES):
-                one = slice(m, m + 1)
+            normed = [early.tile([P, E], F32, name="normed%d" % m) for m in range(TOK_TILES)]
+
+            def statistics(m):
                 for n in range(TILES_PER_CHUNK):
                     nc.vector.bn_stats(out=stats[:, m, n, :], in_=a[m, n][:])
                 nc.vector.bn_aggr(out=mean_var[:, m, :], in_=stats[:, m].rearrange("p n s -> p (n s)"))
-                nc.scalar.activation(out=std[:, one], in_=mean_var[:, m, 1:2], func=ACT.Sqrt, bias=eps[:], scale=1.0)
+                nc.scalar.activation(
+                    out=std[:, m : m + 1], in_=mean_var[:, m, 1:2], func=ACT.Sqrt, bias=eps[:], scale=1.0
+                )
+
+            def normalise(m):
+                one = slice(m, m + 1)
                 nc.vector.reciprocal(out=rstd[:, one], in_=std[:, one])
                 nc.vector.scalar_tensor_tensor(
                     out=shift[:, one], in0=mean_var[:, m, 0:1], scalar=-1.0, in1=rstd[:, one], op0=ALU.mult, op1=ALU.mult
                 )
-                x = early.tile([P, E], F32, name="normed%d" % m)
                 for n in range(TILES_PER_CHUNK):
                     nc.scalar.activation(
-                        out=x[:, n * N_TILE : (n + 1) * N_TILE],
+                        out=normed[m][:, n * N_TILE : (n + 1) * N_TILE],
                         in_=a[m, n][:],
                         func=ACT.Identity,
                         scale=rstd[:, one],
                         bias=shift[:, one],
                     )
-                normed.append(x)
+
+            for m in range(TOK_TILES + 1):
+                if m < TOK_TILES:
+                    statistics(m)
+                if m > 0:
+                    normalise(m - 1)
+
+            copy_weight_unit(GATE, 0, 1)
+            copy_weight_unit(GATE, 1, 1)
+            quantise_weight_tile(GATE, 0)
+            copy_weight_unit(UP, 0, 0)
+            copy_weight_unit(UP, 0, 1)
 
             z_planes = early.tile([P, E_BLOCKS, TOKENS], BF16, name="z_planes")
             for r in range(E_BLOCKS):
                 flipped = bank([P, TOKENS], F32)
                 for m in range(TOK_TILES):
-                    nc.tensor.transpose(
-                        flipped[:, m * P : (m + 1) * P], normed[m][:, r * P : (r + 1) * P], ident_f32[:]
-                    )
+                    nc.tensor.transpose(flipped[:, tokens(m)], normed[m][:, r * P : (r + 1) * P], ident_f32[:])
                 gain = gain_bias[:, r : r + 1]
                 bias = gain_bias[:, E_BLOCKS + r : E_BLOCKS + r + 1]
                 if r % 2 == 0:
@@ -212,38 +255,57 @@ def tile_selfdecoderblock_pb_kernel(tc, h_attn, Wo, gamma2, beta2, Wg, Wu, out):
                         out=z_planes[:, r, :], in0=flipped[:], scalar1=gain, scalar2=bias, op0=ALU.mult, op1=ALU.add
                     )
             nc.scalar.activation(out=warm[:, 1:2], in_=z_planes[:, E_BLOCKS - 2, 0:1], func=ACT.Gelu)
+            z_grouped = []
             for g in range(PASSES):
-                z_grouped = early.tile([P, TOKENS * PACK], BF16, name="z_grouped%d" % g, align_bytes=64)
-                regroup(nc.vector.tensor_copy, z_grouped[:], z_planes[:, g * PACK : (g + 1) * PACK, :])
-                nc.vector.quantize_mx(out=z_codes[:, g, :].bitcast(FP8X4), scales=z_scales[:, g, :], in_=z_grouped[:])
+                grouped = early.tile([P, TOKENS * PACK], BF16, name="z_grouped%d" % g, align_bytes=64)
+                regroup(nc.vector.tensor_copy, grouped[:], z_planes[:, g * PACK : (g + 1) * PACK, :])
+                z_grouped.append(grouped)
+            for g in range(PASSES):
+                quantise_unit(z_grouped[g], z, g, slice(0, TOKENS))
 
-        z = (z_codes, z_scales)
         late = ctx.enter_context(tc.tile_pool(name="late", bufs=1, reuse_waits="tile"))
-        for c in range(CHUNKS):
-            quantised = []
-            for index in (2 * c, 2 * c + 1):
-                quantised.append(quantise_weight_chunk(raws[index]))
-                if index + RAW_BUFS < len(chunk_order):
-                    raws.append(load_gate_or_up(index + RAW_BUFS))
-            wg, wu = quantised
-            gates = {}
-            for i in range(TILES_PER_CHUNK):
-                cols = slice(i * N_TILE, (i + 1) * N_TILE)
-                for m in range(TOK_TILES):
+        gates = {}
+
+        def gate_branch(j):
+            for m in range(TOK_TILES):
+                acc = bank([P, N_TILE], F32)
+                for g in range(PASSES):
+                    product(acc[:], z, tokens(m), moving[GATE, j], slice(0, N_TILE), g)
+                gates[j, m] = late.tile([P, N_TILE], F32, name="gate", bufs=2 * TOK_TILES)
+                nc.scalar.activation(out=gates[j, m][:], in_=acc[:], func=ACT.Gelu)
+
+        def up_branch(j):
+            for pair in range(TOK_TILES // 2):
+                result = late.tile([P, 2, N_TILE], F32, name="result", bufs=4)
+                for half in range(2):
+                    m = 2 * pair + half
                     acc = bank([P, N_TILE], F32)
                     for g in range(PASSES):
-                        product(acc[:], z, slice(m * P, (m + 1) * P), wg, cols, g)
-                    gates[i, m] = late.tile([P, N_TILE], F32, name="gate", bufs=10)
-                    nc.scalar.activation(out=gates[i, m][:], in_=acc[:], func=ACT.Gelu)
-            for i in range(TILES_PER_CHUNK):
-                cols = slice(i * N_TILE, (i + 1) * N_TILE)
-                out_cols = slice(c * CHUNK + i * N_TILE, c * CHUNK + (i + 1) * N_TILE)
-                for pair in range(TOK_TILES // 2):
-                    result = late.tile([P, 2, N_TILE], F32, name="result", bufs=4)
-                    for half in range(2):
-                        m = 2 * pair + half
-                        acc = bank([P, N_TILE], F32)
-                        for g in range(PASSES):
-                            product(acc[:], z, slice(m * P, (m + 1) * P), wu, cols, g)
-                        nc.vector.tensor_tensor(out=result[:, half, :], in0=gates[i, m][:], in1=acc[:], op=ALU.mult)
-                    nc.sync.dma_start(out=out_dram[:, 2 * pair : 2 * pair + 2, out_cols], in_=result[:])
+                        product(acc[:], z, tokens(m), moving[UP, j], slice(0, N_TILE), g)
+                    nc.vector.tensor_tensor(out=result[:, half, :], in0=gates[j, m][:], in1=acc[:], op=ALU.mult)
+                nc.sync.dma_start(
+                    out=out_dram[:, 2 * pair : 2 * pair + 2, j * N_TILE : (j + 1) * N_TILE], in_=result[:]
+                )
+
+        def copy_weight_tiles(j):
+            for b in (GATE, UP):
+                for g in range(PASSES):
+                    copy_weight_unit(b, j, g)
+            if j % TILES_PER_CHUNK == TILES_PER_CHUNK - 1:
+                load_chunks(RAW_BUFS + j + 1)
+
+        copy_weight_unit(GATE, 1, 0)
+        copy_weight_unit(UP, 1, 0)
+        copy_weight_unit(UP, 1, 1)
+        load_chunks(RAW_BUFS + 2)
+        quantise_weight_tile(UP, 0)
+        gate_branch(0)
+        for j in range(F_TILES):
+            if j + 2 < F_TILES:
+                copy_weight_tiles(j + 2)
+            if j + 1 < F_TILES:
+                quantise_weight_tile(GATE, j + 1)
+                quantise_weight_tile(UP, j + 1)
+            up_branch(j)
+            if j + 1 < F_TILES:
+                gate_branch(j + 1)

@@ -52,7 +52,7 @@ def tile_selfdecoderblock_pb_kernel(tc, h_attn, Wo, gamma2, beta2, Wg, Wu, out):
         keep = ctx.enter_context(tc.tile_pool(name="keep", bufs=1))
         raw_pool = ctx.enter_context(tc.tile_pool(name="raw", bufs=RAW_BUFS))
         stage = ctx.enter_context(tc.tile_pool(name="stage", bufs=10))
-        weights = ctx.enter_context(tc.tile_pool(name="weights", bufs=6))
+        weights = ctx.enter_context(tc.tile_pool(name="weights", bufs=8))
         psum = ctx.enter_context(tc.psum_pool(name="psum", bufs=8))
 
         def bank(shape, dtype):
@@ -135,41 +135,18 @@ def tile_selfdecoderblock_pb_kernel(tc, h_attn, Wo, gamma2, beta2, Wg, Wu, out):
         )
 
         with tc.tile_pool(name="early", bufs=1) as early:
+            gb_rows = early.tile([P, P], BF16, name="gb_rows")
+            nc.vector.memset(gb_rows[:], 0.0)
+            nc.sync.dma_start(out=gb_rows[0:E_BLOCKS, :], in_=gamma2.rearrange("(r c) -> r c", c=P))
+            nc.sync.dma_start(out=gb_rows[E_BLOCKS : 2 * E_BLOCKS, :], in_=beta2.rearrange("(r c) -> r c", c=P))
+            wo_raw = load_wo()
             h_rows = []
             for m in range(TOK_TILES):
                 rows = early.tile([P, E], BF16, name="h_rows%d" % m)
                 nc.sync.dma_start(out=rows[:], in_=h_rows_dram[m])
                 h_rows.append(rows)
-            wo_raw = load_wo()
             load_chunks(RAW_BUFS - 1)
-            gb_rows = early.tile([P, P], BF16, name="gb_rows")
-            nc.vector.memset(gb_rows[:], 0.0)
-            nc.scalar.dma_start(out=gb_rows[0:E_BLOCKS, :], in_=gamma2.rearrange("(r c) -> r c", c=P))
-            nc.scalar.dma_start(out=gb_rows[E_BLOCKS : 2 * E_BLOCKS, :], in_=beta2.rearrange("(r c) -> r c", c=P))
             nc.scalar.activation(out=warm[:, 0:1], in_=eps[:], func=ACT.Sqrt)
-
-            h = (
-                early.tile([P, PASSES, TOKENS], U32, name="h_codes", align_bytes=64),
-                early.tile([P, PASSES, TOKENS], U8, name="h_scales", align_bytes=64),
-            )
-            h_grouped = []
-            for m in range(TOK_TILES):
-                words = bank([P, PASSES * 2, P], F32)
-                for q in range(PASSES * 2):
-                    nc.tensor.transpose(
-                        words[:, q, :], h_rows[m][:].bitcast(F32)[:, q * P : (q + 1) * P], ident_f32[:]
-                    )
-                grouped = early.tile([P, PASSES, P * PACK], BF16, name="h_grouped%d" % m, align_bytes=64)
-                nc.scalar.copy(
-                    out=grouped[:].bitcast(F32).rearrange("p g (r u) -> p g r u", u=2),
-                    in_=words[:].rearrange("p (g u) r -> p g r u", u=2),
-                )
-                h_grouped.append(grouped)
-            for m in range(TOK_TILES):
-                for g in range(PASSES):
-                    nc.vector.quantize_mx(
-                        out=h[0][:, g, tokens(m)].bitcast(FP8X4), scales=h[1][:, g, tokens(m)], in_=h_grouped[m][:, g, :]
-                    )
 
             gb_bank = bank([P, P], BF16)
             nc.tensor.transpose(gb_bank[:], gb_rows[:], ident_bf16[:])
@@ -189,15 +166,35 @@ def tile_selfdecoderblock_pb_kernel(tc, h_attn, Wo, gamma2, beta2, Wg, Wu, out):
                 quantise_unit(wo_grouped[g, 0], wo, g, slice(0, N_TILE))
             quantise_unit(wo_grouped[PASSES - 1, 1], wo, PASSES - 1, slice(N_TILE, 2 * N_TILE))
             load_chunks(RAW_BUFS)
-            a = {}
-            for g in range(PASSES):
-                for n in range(TILES_PER_CHUNK):
-                    for m in range(TOK_TILES):
-                        if g == 0:
-                            a[m, n] = bank([P, N_TILE], F32)
-                        product(a[m, n][:], h, tokens(m), wo, slice(n * N_TILE, (n + 1) * N_TILE), g)
 
-            copy_weight_unit(GATE, 0, 0)
+            h = (
+                early.tile([P, PASSES, TOKENS], U32, name="h_codes", align_bytes=64),
+                early.tile([P, PASSES, TOKENS], U8, name="h_scales", align_bytes=64),
+            )
+            h_grouped = []
+            for m in range(TOK_TILES):
+                words = bank([P, PASSES * 2, P], F32)
+                for q in range(PASSES * 2):
+                    nc.tensor.transpose(
+                        words[:, q, :], h_rows[m][:].bitcast(F32)[:, q * P : (q + 1) * P], ident_f32[:]
+                    )
+                grouped = early.tile([P, PASSES, P * PACK], BF16, name="h_grouped%d" % m, align_bytes=64)
+                nc.scalar.copy(
+                    out=grouped[:].bitcast(F32).rearrange("p g (r u) -> p g r u", u=2),
+                    in_=words[:].rearrange("p (g u) r -> p g r u", u=2),
+                )
+                h_grouped.append(grouped)
+
+            a = {}
+            for m in range(TOK_TILES):
+                for g in range(PASSES):
+                    nc.vector.quantize_mx(
+                        out=h[0][:, g, tokens(m)].bitcast(FP8X4), scales=h[1][:, g, tokens(m)], in_=h_grouped[m][:, g, :]
+                    )
+                for n in range(TILES_PER_CHUNK):
+                    a[m, n] = bank([P, N_TILE], F32)
+                    for g in range(PASSES):
+                        product(a[m, n][:], h, tokens(m), wo, slice(n * N_TILE, (n + 1) * N_TILE), g)
 
             stats = early.tile([P, TOK_TILES, TILES_PER_CHUNK, 6], F32, name="stats")
             mean_var = early.tile([P, TOK_TILES, 2], F32, name="mean_var")
@@ -206,62 +203,87 @@ def tile_selfdecoderblock_pb_kernel(tc, h_attn, Wo, gamma2, beta2, Wg, Wu, out):
             shift = early.tile([P, TOK_TILES], F32, name="shift")
             normed = [early.tile([P, E], F32, name="normed%d" % m) for m in range(TOK_TILES)]
 
-            def statistics(m):
+            copy_weight_unit(GATE, 0, 0)
+            copy_weight_unit(GATE, 1, 0)
+            copy_weight_unit(UP, 0, 0)
+            for m in range(TOK_TILES):
                 for n in range(TILES_PER_CHUNK):
                     nc.vector.bn_stats(out=stats[:, m, n, :], in_=a[m, n][:])
                 nc.vector.bn_aggr(out=mean_var[:, m, :], in_=stats[:, m].rearrange("p n s -> p (n s)"))
-                nc.scalar.activation(
-                    out=std[:, m : m + 1], in_=mean_var[:, m, 1:2], func=ACT.Sqrt, bias=eps[:], scale=1.0
-                )
+            copy_weight_unit(GATE, 0, 1)
+            nc.scalar.activation(out=std[:], in_=mean_var[:, :, 1], func=ACT.Sqrt, bias=eps[:], scale=1.0)
+            nc.vector.reciprocal(out=rstd[:], in_=std[:])
+            nc.vector.scalar_tensor_tensor(
+                out=shift[:], in0=mean_var[:, :, 0], scalar=-1.0, in1=rstd[:], op0=ALU.mult, op1=ALU.mult
+            )
 
             def normalise(m):
-                one = slice(m, m + 1)
-                nc.vector.reciprocal(out=rstd[:, one], in_=std[:, one])
-                nc.vector.scalar_tensor_tensor(
-                    out=shift[:, one], in0=mean_var[:, m, 0:1], scalar=-1.0, in1=rstd[:, one], op0=ALU.mult, op1=ALU.mult
-                )
                 for n in range(TILES_PER_CHUNK):
                     nc.scalar.activation(
                         out=normed[m][:, n * N_TILE : (n + 1) * N_TILE],
                         in_=a[m, n][:],
                         func=ACT.Identity,
-                        scale=rstd[:, one],
-                        bias=shift[:, one],
+                        scale=rstd[:, m : m + 1],
+                        bias=shift[:, m : m + 1],
                     )
-
-            for m in range(TOK_TILES + 1):
-                if m < TOK_TILES:
-                    statistics(m)
-                if m > 0:
-                    normalise(m - 1)
-
-            copy_weight_unit(GATE, 0, 1)
-            copy_weight_unit(GATE, 1, 1)
-            quantise_weight_tile(GATE, 0)
-            copy_weight_unit(UP, 0, 0)
-            copy_weight_unit(UP, 0, 1)
 
             z_planes = early.tile([P, E_BLOCKS, TOKENS], BF16, name="z_planes")
-            for r in range(E_BLOCKS):
-                flipped = bank([P, TOKENS], F32)
-                for m in range(TOK_TILES):
-                    nc.tensor.transpose(flipped[:, tokens(m)], normed[m][:, r * P : (r + 1) * P], ident_f32[:])
-                gain = gain_bias[:, r : r + 1]
-                bias = gain_bias[:, E_BLOCKS + r : E_BLOCKS + r + 1]
-                if r % 2 == 0:
-                    nc.scalar.activation(out=z_planes[:, r, :], in_=flipped[:], func=ACT.Identity, scale=gain, bias=bias)
-                else:
-                    nc.vector.tensor_scalar(
-                        out=z_planes[:, r, :], in0=flipped[:], scalar1=gain, scalar2=bias, op0=ALU.mult, op1=ALU.add
-                    )
-            nc.scalar.activation(out=warm[:, 1:2], in_=z_planes[:, E_BLOCKS - 2, 0:1], func=ACT.Gelu)
-            z_grouped = []
-            for g in range(PASSES):
-                grouped = early.tile([P, TOKENS * PACK], BF16, name="z_grouped%d" % g, align_bytes=64)
-                regroup(nc.vector.tensor_copy, grouped[:], z_planes[:, g * PACK : (g + 1) * PACK, :])
-                z_grouped.append(grouped)
-            for g in range(PASSES):
-                quantise_unit(z_grouped[g], z, g, slice(0, TOKENS))
+
+            def half_tokens(q):
+                return slice(q * 2 * P, (q + 1) * 2 * P)
+
+            def flip(q):
+                for first_block in range(0, E_BLOCKS, 2):
+                    flipped = bank([P, 2, 2 * P], F32)
+                    for i in range(2):
+                        r = first_block + i
+                        for tile_in_half in range(2):
+                            nc.tensor.transpose(
+                                flipped[:, i, tokens(tile_in_half)],
+                                normed[2 * q + tile_in_half][:, r * P : (r + 1) * P],
+                                ident_f32[:],
+                            )
+                    for i in range(2):
+                        r = first_block + i
+                        gain = gain_bias[:, r : r + 1]
+                        bias = gain_bias[:, E_BLOCKS + r : E_BLOCKS + r + 1]
+                        if q == 0:
+                            nc.vector.tensor_scalar(
+                                out=z_planes[:, r, half_tokens(q)],
+                                in0=flipped[:, i, :],
+                                scalar1=gain,
+                                scalar2=bias,
+                                op0=ALU.mult,
+                                op1=ALU.add,
+                            )
+                        else:
+                            nc.scalar.activation(
+                                out=z_planes[:, r, half_tokens(q)],
+                                in_=flipped[:, i, :],
+                                func=ACT.Identity,
+                                scale=gain,
+                                bias=bias,
+                            )
+
+            copy_weight_unit(GATE, 1, 1)
+            quantise_weight_tile(GATE, 0)
+            quantise_weight_tile(GATE, 1)
+            normalise(0)
+            normalise(1)
+            flip(0)
+            normalise(2)
+            normalise(3)
+            flip(1)
+            nc.scalar.activation(out=warm[:, 1:2], in_=z_planes[:, E_BLOCKS - 1, TOKENS - 1 : TOKENS], func=ACT.Gelu)
+            for q in range(2):
+                z_grouped = []
+                for g in range(PASSES):
+                    grouped = early.tile([P, 2 * P * PACK], BF16, name="z_grouped%d%d" % (q, g), align_bytes=64)
+                    regroup(nc.vector.tensor_copy, grouped[:], z_planes[:, g * PACK : (g + 1) * PACK, half_tokens(q)])
+                    z_grouped.append(grouped)
+                copy_weight_unit(UP, q, 1)
+                for g in range(PASSES):
+                    quantise_unit(z_grouped[g], z, g, half_tokens(q))
 
         late = ctx.enter_context(tc.tile_pool(name="late", bufs=1, reuse_waits="tile"))
         gates = {}
@@ -294,18 +316,18 @@ def tile_selfdecoderblock_pb_kernel(tc, h_attn, Wo, gamma2, beta2, Wg, Wu, out):
             if j % TILES_PER_CHUNK == TILES_PER_CHUNK - 1:
                 load_chunks(RAW_BUFS + j + 1)
 
-        copy_weight_unit(GATE, 1, 0)
         copy_weight_unit(UP, 1, 0)
-        copy_weight_unit(UP, 1, 1)
         load_chunks(RAW_BUFS + 2)
         quantise_weight_tile(UP, 0)
         gate_branch(0)
+        copy_weight_tiles(2)
+        quantise_weight_tile(UP, 1)
         for j in range(F_TILES):
-            if j + 2 < F_TILES:
-                copy_weight_tiles(j + 2)
-            if j + 1 < F_TILES:
-                quantise_weight_tile(GATE, j + 1)
-                quantise_weight_tile(UP, j + 1)
             up_branch(j)
             if j + 1 < F_TILES:
                 gate_branch(j + 1)
+            if j + 3 < F_TILES:
+                copy_weight_tiles(j + 3)
+            if j + 2 < F_TILES:
+                quantise_weight_tile(GATE, j + 2)
+                quantise_weight_tile(UP, j + 2)

@@ -29,6 +29,8 @@ EPS = 1e-6
 RAW_BUFS = 5
 GATE = 0
 UP = 1
+GPSIMD_COLS = 256
+FIRST_SHARED_TILE = 3
 
 FLOPS = 2 * TOKENS * E * (E + 2 * F)
 
@@ -44,7 +46,6 @@ def tile_selfdecoderblock_pb_kernel(tc, h_attn, Wo, gamma2, beta2, Wg, Wu, out):
     nc = tc.nc
     h_rows_dram = h_attn.rearrange("b s h d -> b s (h d)")
     wo_dram = Wo.rearrange("h d e -> (h d) e")
-    out_dram = out.rearrange("b s f -> s b f")
     chunk_order = [(w, c) for c in range(F // CHUNK) for w in (Wg, Wu)]
 
     with ExitStack() as ctx:
@@ -106,21 +107,36 @@ def tile_selfdecoderblock_pb_kernel(tc, h_attn, Wo, gamma2, beta2, Wg, Wu, out):
         def tokens(m):
             return slice(m * P, (m + 1) * P)
 
-        grouped_units = {}
+        pieces = {}
         moving = {}
+
+        def copy_weight_piece(copy, grouped, b, j, g, first, width):
+            raw = raws[2 * (j // TILES_PER_CHUNK) + b]
+            start = (j % TILES_PER_CHUNK) * N_TILE + first
+            regroup(copy, grouped[:], raw[:, g, :, start : start + width])
+            pieces[b, j] = pieces.get((b, j), []) + [(grouped, g, first, width)]
 
         def copy_weight_unit(b, j, g):
             copy = nc.scalar.copy if g == 0 else nc.vector.tensor_copy
-            raw = raws[2 * (j // TILES_PER_CHUNK) + b]
-            grouped_units[b, j, g] = copy_unit(copy, raw, g, j % TILES_PER_CHUNK)
+            shared = b == UP and g == 1 and j >= FIRST_SHARED_TILE
+            width = N_TILE - GPSIMD_COLS if shared else N_TILE
+            grouped = stage.tile([P, width * PACK], BF16, name="grouped", align_bytes=64)
+            copy_weight_piece(copy, grouped, b, j, g, 0, width)
+
+        def gpsimd_copy(out, in_):
+            nc.gpsimd.tensor_scalar(out=out, in0=in_, scalar1=1.0, scalar2=0.0, op0=ALU.mult, op1=ALU.add)
+
+        def copy_gpsimd_share(j):
+            grouped = stage.tile([P, GPSIMD_COLS * PACK], BF16, name="grouped_by_gpsimd", bufs=1, align_bytes=64)
+            copy_weight_piece(gpsimd_copy, grouped, UP, j, 1, N_TILE - GPSIMD_COLS, GPSIMD_COLS)
 
         def quantise_weight_tile(b, j):
             moving[b, j] = (
                 weights.tile([P, PASSES, N_TILE], U32, name="codes", align_bytes=64),
                 weights.tile([P, PASSES, N_TILE], U8, name="scales", align_bytes=64),
             )
-            for g in range(PASSES):
-                quantise_unit(grouped_units[b, j, g], moving[b, j], g, slice(0, N_TILE))
+            for grouped, g, first, width in pieces[b, j]:
+                quantise_unit(grouped, moving[b, j], g, slice(first, first + width))
 
         ident_f32 = keep.tile([P, P], F32, name="ident_f32")
         make_identity(nc, ident_f32[:])
@@ -297,17 +313,13 @@ def tile_selfdecoderblock_pb_kernel(tc, h_attn, Wo, gamma2, beta2, Wg, Wu, out):
                 nc.scalar.activation(out=gates[j, m][:], in_=acc[:], func=ACT.Gelu)
 
         def up_branch(j):
-            for pair in range(TOK_TILES // 2):
-                result = late.tile([P, 2, N_TILE], F32, name="result", bufs=4)
-                for half in range(2):
-                    m = 2 * pair + half
-                    acc = bank([P, N_TILE], F32)
-                    for g in range(PASSES):
-                        product(acc[:], z, tokens(m), moving[UP, j], slice(0, N_TILE), g)
-                    nc.vector.tensor_tensor(out=result[:, half, :], in0=gates[j, m][:], in1=acc[:], op=ALU.mult)
-                nc.sync.dma_start(
-                    out=out_dram[:, 2 * pair : 2 * pair + 2, j * N_TILE : (j + 1) * N_TILE], in_=result[:]
-                )
+            for m in range(TOK_TILES):
+                acc = bank([P, N_TILE], F32)
+                for g in range(PASSES):
+                    product(acc[:], z, tokens(m), moving[UP, j], slice(0, N_TILE), g)
+                result = late.tile([P, N_TILE], F32, name="result", bufs=2 * TOK_TILES)
+                nc.vector.tensor_tensor(out=result[:], in0=gates[j, m][:], in1=acc[:], op=ALU.mult)
+                nc.sync.dma_start(out=out[m, :, j * N_TILE : (j + 1) * N_TILE], in_=result[:])
 
         def copy_weight_tiles(j):
             for b in (GATE, UP):
@@ -324,6 +336,8 @@ def tile_selfdecoderblock_pb_kernel(tc, h_attn, Wo, gamma2, beta2, Wg, Wu, out):
         quantise_weight_tile(UP, 1)
         for j in range(F_TILES):
             up_branch(j)
+            if FIRST_SHARED_TILE <= j + 2 < F_TILES:
+                copy_gpsimd_share(j + 2)
             if j + 1 < F_TILES:
                 gate_branch(j + 1)
             if j + 3 < F_TILES:

from contextlib import ExitStack

import concourse.mybir as mybir
from concourse.masks import make_identity

F32 = mybir.dt.float32
BF16 = mybir.dt.bfloat16
U32 = mybir.dt.uint32
U8 = mybir.dt.uint8
FP8X4 = mybir.dt.float8_e4m3fn_x4
ACT = mybir.ActivationFunctionType
ALU = mybir.AluOpType

P = 128
PACK = 4
K_PASS = P * PACK
TOKENS = 512
TOK_TILES = TOKENS // P
E = 1024
F = 4096
PASSES = E // K_PASS
N_TILE = 512
CHUNK = 1024
TILES_PER_CHUNK = CHUNK // N_TILE
F_TILES = F // N_TILE
E_BLOCKS = E // P
RUN = 4
EPS = 1e-6
RAW_BUFS = 5
GATE = 0
UP = 1
GPSIMD_COLS = 256
FIRST_SHARED_TILE = 3

FLOPS = 2 * TOKENS * E * (E + 2 * F)


def regroup(copy, grouped, rows):
    copy(
        out=grouped.rearrange("p (c i t) -> p c t i", i=RUN, t=PACK),
        in_=rows.rearrange("p t (c i) -> p c t i", i=RUN),
    )


def tile_selfdecoderblock_pb_kernel(tc, h_attn, Wo, gamma2, beta2, Wg, Wu, out):
    nc = tc.nc
    h_rows_dram = h_attn.rearrange("b s h d -> b s (h d)")
    wo_dram = Wo.rearrange("h d e -> (h d) e")
    chunk_order = [(w, c) for c in range(F // CHUNK) for w in (Wg, Wu)]

    with ExitStack() as ctx:
        ctx.enter_context(tc.manual_schedule())
        keep = ctx.enter_context(tc.tile_pool(name="keep", bufs=1))
        raw_pool = ctx.enter_context(tc.tile_pool(name="raw", bufs=RAW_BUFS))
        stage = ctx.enter_context(tc.tile_pool(name="stage", bufs=10))
        weights = ctx.enter_context(tc.tile_pool(name="weights", bufs=8))
        psum = ctx.enter_context(tc.psum_pool(name="psum", bufs=8))

        def bank(shape, dtype):
            return psum.tile(shape, dtype, name="bank")

        def load_wo():
            raw = raw_pool.tile([P, PASSES, PACK, CHUNK], BF16, name="raw")
            for g in range(PASSES):
                for u in range(2):
                    first = g * K_PASS + u * 2 * P
                    nc.sync.dma_start(
                        out=raw[:, g, 2 * u : 2 * u + 2, :],
                        in_=wo_dram[first : first + 2 * P, :].rearrange("(p e) n -> p e n", e=2),
                    )
            return raw

        raws = []

        def load_chunks(count):
            for w, c in chunk_order[len(raws) : count]:
                raw = raw_pool.tile([P, PASSES, PACK, CHUNK], BF16, name="raw")
                for g in range(PASSES):
                    nc.sync.dma_start(
                        out=raw[:, g],
                        in_=w[g * K_PASS : (g + 1) * K_PASS, c * CHUNK : (c + 1) * CHUNK].rearrange(
                            "(t p) n -> p t n", p=P
                        ),
                    )
                raws.append(raw)

        def copy_unit(copy, raw, g, tile_in_chunk):
            grouped = stage.tile([P, N_TILE * PACK], BF16, name="grouped", align_bytes=64)
            regroup(copy, grouped[:], raw[:, g, :, tile_in_chunk * N_TILE : (tile_in_chunk + 1) * N_TILE])
            return grouped

        def quantise_unit(grouped, operand, g, cols):
            codes, scales = operand
            nc.vector.quantize_mx(out=codes[:, g, cols].bitcast(FP8X4), scales=scales[:, g, cols], in_=grouped[:])

        def product(acc, left, left_cols, right, right_cols, g):
            nc.tensor.matmul_mx(
                out=acc,
                lhsT=left[0][:, g, left_cols].bitcast(FP8X4),
                lhsT_scale=left[1][:, g, left_cols],
                rhs=right[0][:, g, right_cols].bitcast(FP8X4),
                rhs_scale=right[1][:, g, right_cols],
                start=(g == 0),
                stop=(g == PASSES - 1),
            )

        def tokens(m):
            return slice(m * P, (m + 1) * P)

        pieces = {}
        moving = {}

        def copy_weight_piece(copy, grouped, b, j, g, first, width):
            raw = raws[2 * (j // TILES_PER_CHUNK) + b]
            start = (j % TILES_PER_CHUNK) * N_TILE + first
            regroup(copy, grouped[:], raw[:, g, :, start : start + width])
            pieces[b, j] = pieces.get((b, j), []) + [(grouped, g, first, width)]

        def copy_weight_unit(b, j, g):
            copy = nc.scalar.copy if g == 0 else nc.vector.tensor_copy
            shared = b == UP and g == 1 and j >= FIRST_SHARED_TILE
            width = N_TILE - GPSIMD_COLS if shared else N_TILE
            grouped = stage.tile([P, width * PACK], BF16, name="grouped", align_bytes=64)
            copy_weight_piece(copy, grouped, b, j, g, 0, width)

        def gpsimd_copy(out, in_):
            nc.gpsimd.tensor_scalar(out=out, in0=in_, scalar1=1.0, scalar2=0.0, op0=ALU.mult, op1=ALU.add)

        def copy_gpsimd_share(j):
            grouped = stage.tile([P, GPSIMD_COLS * PACK], BF16, name="grouped_by_gpsimd", bufs=1, align_bytes=64)
            copy_weight_piece(gpsimd_copy, grouped, UP, j, 1, N_TILE - GPSIMD_COLS, GPSIMD_COLS)

        def quantise_weight_tile(b, j):
            moving[b, j] = (
                weights.tile([P, PASSES, N_TILE], U32, name="codes", align_bytes=64),
                weights.tile([P, PASSES, N_TILE], U8, name="scales", align_bytes=64),
            )
            for grouped, g, first, width in pieces[b, j]:
                quantise_unit(grouped, moving[b, j], g, slice(first, first + width))

        ident_f32 = keep.tile([P, P], F32, name="ident_f32")
        make_identity(nc, ident_f32[:])
        ident_bf16 = keep.tile([P, P], BF16, name="ident_bf16")
        make_identity(nc, ident_bf16[:])
        eps = keep.tile([P, 1], F32, name="eps")
        nc.vector.memset(eps[:], EPS)
        warm = keep.tile([P, 2], F32, name="warm")
        z = (
            keep.tile([P, PASSES, TOKENS], U32, name="z_codes", align_bytes=64),
            keep.tile([P, PASSES, TOKENS], U8, name="z_scales", align_bytes=64),
        )

        with tc.tile_pool(name="early", bufs=1) as early:
            gb_rows = early.tile([P, P], BF16, name="gb_rows")
            nc.vector.memset(gb_rows[:], 0.0)
            nc.sync.dma_start(out=gb_rows[0:E_BLOCKS, :], in_=gamma2.rearrange("(r c) -> r c", c=P))
            nc.sync.dma_start(out=gb_rows[E_BLOCKS : 2 * E_BLOCKS, :], in_=beta2.rearrange("(r c) -> r c", c=P))
            wo_raw = load_wo()
            h_rows = []
            for m in range(TOK_TILES):
                rows = early.tile([P, E], BF16, name="h_rows%d" % m)
                nc.sync.dma_start(out=rows[:], in_=h_rows_dram[m])
                h_rows.append(rows)
            load_chunks(RAW_BUFS - 1)
            nc.scalar.activation(out=warm[:, 0:1], in_=eps[:], func=ACT.Sqrt)

            gb_bank = bank([P, P], BF16)
            nc.tensor.transpose(gb_bank[:], gb_rows[:], ident_bf16[:])
            gain_bias = early.tile([P, 2 * E_BLOCKS], F32, name="gain_bias")
            nc.vector.tensor_copy(out=gain_bias[:], in_=gb_bank[:, 0 : 2 * E_BLOCKS])

            wo = (
                early.tile([P, PASSES, E], U32, name="wo_codes", align_bytes=64),
                early.tile([P, PASSES, E], U8, name="wo_scales", align_bytes=64),
            )
            wo_grouped = {}
            for g in range(PASSES):
                wo_grouped[g, 0] = copy_unit(nc.vector.tensor_copy, wo_raw, g, 0)
                wo_grouped[g, 1] = copy_unit(nc.scalar.copy, wo_raw, g, 1)
                if g > 0:
                    quantise_unit(wo_grouped[g - 1, 1], wo, g - 1, slice(N_TILE, 2 * N_TILE))
                quantise_unit(wo_grouped[g, 0], wo, g, slice(0, N_TILE))
            quantise_unit(wo_grouped[PASSES - 1, 1], wo, PASSES - 1, slice(N_TILE, 2 * N_TILE))
            load_chunks(RAW_BUFS)

            h = (
                early.tile([P, PASSES, TOKENS], U32, name="h_codes", align_bytes=64),
                early.tile([P, PASSES, TOKENS], U8, name="h_scales", align_bytes=64),
            )
            h_grouped = []
            for m in range(TOK_TILES):
                words = bank([P, PASSES * 2, P], F32)
                for q in range(PASSES * 2):
                    nc.tensor.transpose(
                        words[:, q, :], h_rows[m][:].bitcast(F32)[:, q * P : (q + 1) * P], ident_f32[:]
                    )
                grouped = early.tile([P, PASSES, P * PACK], BF16, name="h_grouped%d" % m, align_bytes=64)
                nc.scalar.copy(
                    out=grouped[:].bitcast(F32).rearrange("p g (r u) -> p g r u", u=2),
                    in_=words[:].rearrange("p (g u) r -> p g r u", u=2),
                )
                h_grouped.append(grouped)

            a = {}
            for m in range(TOK_TILES):
                for g in range(PASSES):
                    nc.vector.quantize_mx(
                        out=h[0][:, g, tokens(m)].bitcast(FP8X4), scales=h[1][:, g, tokens(m)], in_=h_grouped[m][:, g, :]
                    )
                for n in range(TILES_PER_CHUNK):
                    a[m, n] = bank([P, N_TILE], F32)
                    for g in range(PASSES):
                        product(a[m, n][:], h, tokens(m), wo, slice(n * N_TILE, (n + 1) * N_TILE), g)

            stats = early.tile([P, TOK_TILES, TILES_PER_CHUNK, 6], F32, name="stats")
            mean_var = early.tile([P, TOK_TILES, 2], F32, name="mean_var")
            std = early.tile([P, TOK_TILES], F32, name="std")
            rstd = early.tile([P, TOK_TILES], F32, name="rstd")
            shift = early.tile([P, TOK_TILES], F32, name="shift")
            normed = [early.tile([P, E], F32, name="normed%d" % m) for m in range(TOK_TILES)]

            copy_weight_unit(GATE, 0, 0)
            copy_weight_unit(GATE, 1, 0)
            copy_weight_unit(UP, 0, 0)
            for m in range(TOK_TILES):
                for n in range(TILES_PER_CHUNK):
                    nc.vector.bn_stats(out=stats[:, m, n, :], in_=a[m, n][:])
                nc.vector.bn_aggr(out=mean_var[:, m, :], in_=stats[:, m].rearrange("p n s -> p (n s)"))
            copy_weight_unit(GATE, 0, 1)
            nc.scalar.activation(out=std[:], in_=mean_var[:, :, 1], func=ACT.Sqrt, bias=eps[:], scale=1.0)
            nc.vector.reciprocal(out=rstd[:], in_=std[:])
            nc.vector.scalar_tensor_tensor(
                out=shift[:], in0=mean_var[:, :, 0], scalar=-1.0, in1=rstd[:], op0=ALU.mult, op1=ALU.mult
            )

            def normalise(m):
                for n in range(TILES_PER_CHUNK):
                    nc.scalar.activation(
                        out=normed[m][:, n * N_TILE : (n + 1) * N_TILE],
                        in_=a[m, n][:],
                        func=ACT.Identity,
                        scale=rstd[:, m : m + 1],
                        bias=shift[:, m : m + 1],
                    )

            z_planes = early.tile([P, E_BLOCKS, TOKENS], BF16, name="z_planes")

            def half_tokens(q):
                return slice(q * 2 * P, (q + 1) * 2 * P)

            def flip(q):
                for first_block in range(0, E_BLOCKS, 2):
                    flipped = bank([P, 2, 2 * P], F32)
                    for i in range(2):
                        r = first_block + i
                        for tile_in_half in range(2):
                            nc.tensor.transpose(
                                flipped[:, i, tokens(tile_in_half)],
                                normed[2 * q + tile_in_half][:, r * P : (r + 1) * P],
                                ident_f32[:],
                            )
                    for i in range(2):
                        r = first_block + i
                        gain = gain_bias[:, r : r + 1]
                        bias = gain_bias[:, E_BLOCKS + r : E_BLOCKS + r + 1]
                        if q == 0:
                            nc.vector.tensor_scalar(
                                out=z_planes[:, r, half_tokens(q)],
                                in0=flipped[:, i, :],
                                scalar1=gain,
                                scalar2=bias,
                                op0=ALU.mult,
                                op1=ALU.add,
                            )
                        else:
                            nc.scalar.activation(
                                out=z_planes[:, r, half_tokens(q)],
                                in_=flipped[:, i, :],
                                func=ACT.Identity,
                                scale=gain,
                                bias=bias,
                            )

            copy_weight_unit(GATE, 1, 1)
            quantise_weight_tile(GATE, 0)
            quantise_weight_tile(GATE, 1)
            normalise(0)
            normalise(1)
            flip(0)
            normalise(2)
            normalise(3)
            flip(1)
            nc.scalar.activation(out=warm[:, 1:2], in_=z_planes[:, E_BLOCKS - 1, TOKENS - 1 : TOKENS], func=ACT.Gelu)
            for q in range(2):
                z_grouped = []
                for g in range(PASSES):
                    grouped = early.tile([P, 2 * P * PACK], BF16, name="z_grouped%d%d" % (q, g), align_bytes=64)
                    regroup(nc.vector.tensor_copy, grouped[:], z_planes[:, g * PACK : (g + 1) * PACK, half_tokens(q)])
                    z_grouped.append(grouped)
                copy_weight_unit(UP, q, 1)
                for g in range(PASSES):
                    quantise_unit(z_grouped[g], z, g, half_tokens(q))

        late = ctx.enter_context(tc.tile_pool(name="late", bufs=1, reuse_waits="tile"))
        gates = {}

        def gate_branch(j):
            for m in range(TOK_TILES):
                acc = bank([P, N_TILE], F32)
                for g in range(PASSES):
                    product(acc[:], z, tokens(m), moving[GATE, j], slice(0, N_TILE), g)
                gates[j, m] = late.tile([P, N_TILE], F32, name="gate", bufs=2 * TOK_TILES)
                nc.scalar.activation(out=gates[j, m][:], in_=acc[:], func=ACT.Gelu)

        def up_branch(j):
            for m in range(TOK_TILES):
                acc = bank([P, N_TILE], F32)
                for g in range(PASSES):
                    product(acc[:], z, tokens(m), moving[UP, j], slice(0, N_TILE), g)
                result = late.tile([P, N_TILE], F32, name="result", bufs=2 * TOK_TILES)
                nc.vector.tensor_tensor(out=result[:], in0=gates[j, m][:], in1=acc[:], op=ALU.mult)
                nc.sync.dma_start(out=out[m, :, j * N_TILE : (j + 1) * N_TILE], in_=result[:])

        def copy_weight_tiles(j):
            for b in (GATE, UP):
                for g in range(PASSES):
                    copy_weight_unit(b, j, g)
            if j % TILES_PER_CHUNK == TILES_PER_CHUNK - 1:
                load_chunks(RAW_BUFS + j + 1)

        copy_weight_unit(UP, 1, 0)
        load_chunks(RAW_BUFS + 2)
        quantise_weight_tile(UP, 0)
        gate_branch(0)
        copy_weight_tiles(2)
        quantise_weight_tile(UP, 1)
        for j in range(F_TILES):
            up_branch(j)
            if FIRST_SHARED_TILE <= j + 2 < F_TILES:
                copy_gpsimd_share(j + 2)
            if j + 1 < F_TILES:
                gate_branch(j + 1)
            if j + 3 < F_TILES:
                copy_weight_tiles(j + 3)
            if j + 2 < F_TILES:
                quantise_weight_tile(GATE, j + 2)
                quantise_weight_tile(UP, j + 2)
